import numpy as np
import ml_dtypes


def mxq(x, axis, fmt="e4m3"):
    dtype, down = {"e4m3": (ml_dtypes.float8_e4m3fn, 7), "e5m2": (ml_dtypes.float8_e5m2, 14)}[fmt]
    v = np.moveaxis(np.asarray(x, np.float32).astype(ml_dtypes.bfloat16).astype(np.float64), axis, -1)
    blocks = v.reshape(v.shape[:-1] + (-1, 32))
    amax = np.abs(blocks).max(-1, keepdims=True)
    byte = np.maximum(np.where(amax > 0, np.frexp(amax)[1] - 1 + 127, 0) - down, 1)
    scale = np.exp2(byte - 127.0)
    codes = (blocks / scale).astype(np.float32).astype(dtype).astype(np.float64)
    return np.moveaxis((codes * scale).reshape(v.shape), -1, axis)


WIDE = False


def mx_kscale(k):
    if not WIDE:
        return np.ones(k)
    levels = np.array([10, -10, 5, -5, 0])
    a = np.random.permutation(np.resize(levels, k // 512 * 4)).reshape(k // 512, 4)
    idx = np.arange(k)
    return np.exp2(a[idx // 512, idx % 128 // 32])


BF16 = ml_dtypes.bfloat16


def bf(x):
    return np.asarray(x, np.float32).astype(BF16)


def f64(x):
    return np.asarray(x).astype(np.float64)


B, T, C, H, W = 1, 4096, 512, 4, 512
D = C // H
HALF = D // 2
ROPE_BASE = 10000.0


def rotate_half(u):
    return np.concatenate([-u[..., HALF:], u[..., :HALF]], axis=-1)


def setup_inputs():
    s = mx_kscale(C)
    start = np.random.randint(0, T)
    inv_freq = 1.0 / (ROPE_BASE ** (np.arange(0, D, 2) / D))
    freqs = np.outer(start + np.arange(T), inv_freq)
    emb = np.concatenate([freqs, freqs], axis=-1)
    return {"x": bf(np.random.standard_normal((B, T, C)) * s),
            "freqs_cos": bf(np.cos(emb)),
            "freqs_sin": bf(np.sin(emb)),
            "w_attn": bf(np.random.standard_normal((C, 3 * C)) * 1.25 / np.sqrt(C) / s[:, None])}


def reference(x, freqs_cos, freqs_sin, w_attn):
    qkv = mxq(f64(x), 2, "e4m3") @ mxq(f64(w_attn), 0, "e4m3")
    q, k, v = np.split(qkv, 3, axis=-1)
    q = q.reshape(B, T, H, D).transpose(0, 2, 1, 3)
    k = k.reshape(B, T, H, D).transpose(0, 2, 1, 3)
    v = v.reshape(B, T, H, D).transpose(0, 2, 1, 3)
    cos = f64(freqs_cos)[None, None, :, :]
    sin = f64(freqs_sin)[None, None, :, :]
    q_rot = q * cos + rotate_half(q) * sin
    k_rot = k * cos + rotate_half(k) * sin
    return q_rot, k_rot, v

@@ -1,0 +1,184 @@
+from contextlib import ExitStack
+
+import concourse.mybir as mybir
+from concourse.masks import make_identity
+
+F32 = mybir.dt.float32
+BF16 = mybir.dt.bfloat16
+U32 = mybir.dt.uint32
+U8 = mybir.dt.uint8
+FP8X4 = mybir.dt.float8_e4m3fn_x4
+MULT = mybir.AluOpType.mult
+ADD = mybir.AluOpType.add
+SUBTRACT = mybir.AluOpType.subtract
+
+P = 128
+T = 4096
+C = 512
+PACK = 4
+HEADS = 4
+D = 128
+HALF = D // 2
+QK_HEADS = 2 * HEADS
+BANK = 512
+
+ROUNDS = T // P
+GROUP = 4
+GROUPS = ROUNDS // GROUP
+PAIR = 2
+
+FLOPS = 2 * T * C * 3 * C
+
+
+def tile_swaattention_pa_t_kernel(tc, x, freqs_cos, freqs_sin, w_attn, out_0, out_1, out_2):
+    nc = tc.nc
+
+    x_view = x.rearrange("b (p g j) c -> (b p) g (j c)", g=GROUPS, j=GROUP)
+    cos_view = freqs_cos.rearrange("(p g j) d -> p g j d", g=GROUPS, j=GROUP)
+    sin_view = freqs_sin.rearrange("(p g j) d -> p g j d", g=GROUPS, j=GROUP)
+    q_view = out_0.rearrange("b h (p g j) d -> p g (b h) j d", g=GROUPS, j=GROUP)
+    k_view = out_1.rearrange("b h (p g j) d -> p g (b h) j d", g=GROUPS, j=GROUP)
+    v_view = out_2.rearrange("b h (p g j) d -> p g (b h) j d", g=GROUPS, j=GROUP)
+
+    with ExitStack() as ctx:
+        ctx.enter_context(tc.manual_schedule())
+        const = ctx.enter_context(tc.tile_pool(name="const", bufs=1))
+        inputs = ctx.enter_context(tc.tile_pool(name="inputs", bufs=GROUPS))
+        xq = ctx.enter_context(tc.tile_pool(name="xq", bufs=2))
+        results = ctx.enter_context(tc.tile_pool(name="results", bufs=3))
+        psum_t = ctx.enter_context(tc.psum_pool(name="psum_t", bufs=2))
+        psum_mm = ctx.enter_context(tc.psum_pool(name="psum_mm", bufs=2))
+
+        w_raw = const.tile([P, PACK, 3 * C], BF16)
+        nc.sync.dma_start(
+            out=w_raw[:].rearrange("p (u e) c -> p u (e c)", u=2),
+            in_=w_attn.rearrange("(u p e) c -> p u (e c)", u=2, p=P, e=2),
+        )
+        x_in = []
+        cos_in = []
+        sin_in = []
+        for g in range(GROUPS):
+            x_g = inputs.tile([P, GROUP * C], BF16, name="x_g")
+            nc.sync.dma_start(out=x_g[:], in_=x_view[:, g, :])
+            cos_g = inputs.tile([P, GROUP, D], BF16, name="cos_g")
+            nc.sync.dma_start(out=cos_g[:], in_=cos_view[:, g])
+            sin_g = inputs.tile([P, GROUP, D], BF16, name="sin_g")
+            nc.sync.dma_start(out=sin_g[:], in_=sin_view[:, g])
+            x_in.append(x_g)
+            cos_in.append(cos_g)
+            sin_in.append(sin_g)
+
+        identity = const.tile([P, P], F32)
+        make_identity(nc, identity[:])
+
+        def transpose_group(g):
+            x_words = x_in[g][:].bitcast(F32)
+            grouped = xq.tile([P, GROUP * P * PACK], BF16, name="grouped", align_bytes=64)
+            grouped_words = grouped[:].bitcast(F32).rearrange(
+                "p (j r u) -> p j r u", j=GROUP, r=P, u=2
+            )
+            for half_group in range(GROUP // 2):
+                turned = psum_t.tile([P, 2, 2, P], F32, name="turned")
+                for i in range(2):
+                    j = 2 * half_group + i
+                    for u in range(2):
+                        first = (2 * j + u) * P
+                        nc.tensor.transpose(turned[:, i, u, :], x_words[:, first : first + P], identity[:])
+                nc.scalar.copy(
+                    out=grouped_words[:, 2 * half_group : 2 * half_group + 2],
+                    in_=turned[:].rearrange("p i u r -> p i r u"),
+                )
+            return grouped
+
+        def quantise_group(grouped):
+            x_codes = xq.tile([P, GROUP * P], U32, name="x_codes", align_bytes=64)
+            x_scales = xq.tile([P, GROUP * P], U8, name="x_scales", align_bytes=64)
+            nc.vector.quantize_mx(out=x_codes[:].bitcast(FP8X4), scales=x_scales[:], in_=grouped[:])
+            return x_codes, x_scales
+
+        w_grouped = const.tile([P, 3 * BANK * PACK], BF16, align_bytes=64)
+        w_codes = const.tile([P, 3 * BANK], U32, align_bytes=64)
+        w_scales = const.tile([P, 3 * BANK], U8, align_bytes=64)
+        qk_halves = w_raw[:, :, 0 : 2 * C].rearrange("p t (n f d) -> p f n d t", f=2, d=HALF)
+
+        grouped_next = transpose_group(0)
+        for f in range(2):
+            nc.vector.tensor_copy(
+                out=w_grouped[:, f * BANK * PACK : (f + 1) * BANK * PACK].rearrange(
+                    "p (n d t) -> p n d t", n=QK_HEADS, d=HALF
+                ),
+                in_=qk_halves[:, f],
+            )
+        nc.scalar.copy(
+            out=w_grouped[:, 2 * BANK * PACK : 3 * BANK * PACK].rearrange("p (c t) -> p c t", t=PACK),
+            in_=w_raw[:, :, 2 * C : 3 * C].rearrange("p t c -> p c t"),
+        )
+        for block in (0, 1):
+            nc.vector.quantize_mx(
+                out=w_codes[:, block * BANK : (block + 1) * BANK].bitcast(FP8X4),
+                scales=w_scales[:, block * BANK : (block + 1) * BANK],
+                in_=w_grouped[:, block * BANK * PACK : (block + 1) * BANK * PACK],
+            )
+        codes_next = quantise_group(grouped_next)
+        nc.vector.quantize_mx(
+            out=w_codes[:, 2 * BANK : 3 * BANK].bitcast(FP8X4),
+            scales=w_scales[:, 2 * BANK : 3 * BANK],
+            in_=w_grouped[:, 2 * BANK * PACK : 3 * BANK * PACK],
+        )
+
+        for g in range(GROUPS):
+            x_codes, x_scales = codes_next
+            if g + 1 < GROUPS:
+                grouped_next = transpose_group(g + 1)
+            cos_g = cos_in[g]
+            sin_g = sin_in[g]
+            qk_main = results.tile([P, QK_HEADS, GROUP, D], F32, name="qk_main")
+            v_out = results.tile([P, HEADS, GROUP, D], F32, name="v_out")
+            for j in range(GROUP):
+                if j % PAIR == 0:
+                    qk_cross = results.tile([P, QK_HEADS, PAIR, D], F32, name="qk_cross")
+                i = j % PAIR
+                banks = []
+                for block in range(3):
+                    acc = psum_mm.tile([P, BANK], F32, name="acc%d" % block)
+                    nc.tensor.matmul_mx(
+                        out=acc[:],
+                        lhsT=x_codes[:, j * P : (j + 1) * P].bitcast(FP8X4),
+                        lhsT_scale=x_scales[:, j * P : (j + 1) * P],
+                        rhs=w_codes[:, block * BANK : (block + 1) * BANK].bitcast(FP8X4),
+                        rhs_scale=w_scales[:, block * BANK : (block + 1) * BANK],
+                        start=True,
+                        stop=True,
+                    )
+                    banks.append(acc)
+                low = banks[0][:].rearrange("p (n d) -> p n d", d=HALF)
+                high = banks[1][:].rearrange("p (n d) -> p n d", d=HALF)
+
+                def table(tab, first):
+                    return tab[:, j : j + 1, first : first + HALF].to_broadcast([P, QK_HEADS, HALF])
+
+                nc.vector.tensor_tensor(out=qk_main[:, :, j, 0:HALF], in0=low, in1=table(cos_g, 0), op=MULT)
+                nc.vector.tensor_tensor(out=qk_cross[:, :, i, HALF:D], in0=low, in1=table(sin_g, HALF), op=MULT)
+                nc.vector.tensor_tensor(out=qk_main[:, :, j, HALF:D], in0=high, in1=table(cos_g, HALF), op=MULT)
+                nc.vector.tensor_tensor(out=qk_cross[:, :, i, 0:HALF], in0=high, in1=table(sin_g, 0), op=MULT)
+                nc.scalar.copy(out=v_out[:, :, j, :], in_=banks[2][:].rearrange("p (h d) -> p h d", d=D))
+
+                if j == 1 and g + 1 < GROUPS:
+                    codes_next = quantise_group(grouped_next)
+                if i == PAIR - 1:
+                    rounds = slice(j + 1 - PAIR, j + 1)
+                    nc.gpsimd.tensor_tensor(
+                        out=qk_main[:, :, rounds, 0:HALF],
+                        in0=qk_main[:, :, rounds, 0:HALF],
+                        in1=qk_cross[:, :, :, 0:HALF],
+                        op=SUBTRACT,
+                    )
+                    nc.gpsimd.tensor_tensor(
+                        out=qk_main[:, :, rounds, HALF:D],
+                        in0=qk_main[:, :, rounds, HALF:D],
+                        in1=qk_cross[:, :, :, HALF:D],
+                        op=ADD,
+                    )
+            nc.sync.dma_start(out=v_view[:, g], in_=v_out[:])
+            nc.sync.dma_start(out=q_view[:, g], in_=qk_main[:, 0:HEADS])
+            nc.sync.dma_start(out=k_view[:, g], in_=qk_main[:, HEADS:QK_HEADS])

@@ -127,58 +127,64 @@ def tile_swaattention_pa_t_kernel(tc, x, freqs_cos, freqs_sin, w_attn, out_0, ou
         )
 
         for g in range(GROUPS):
+            last_group = g == GROUPS - 1
             x_codes, x_scales = codes_next
-            if g + 1 < GROUPS:
+            if not last_group:
                 grouped_next = transpose_group(g + 1)
             cos_g = cos_in[g]
             sin_g = sin_in[g]
             qk_main = results.tile([P, QK_HEADS, GROUP, D], F32, name="qk_main")
             v_out = results.tile([P, HEADS, GROUP, D], F32, name="v_out")
-            for j in range(GROUP):
-                if j % PAIR == 0:
-                    qk_cross = results.tile([P, QK_HEADS, PAIR, D], F32, name="qk_cross")
-                i = j % PAIR
-                banks = []
-                for block in range(3):
-                    acc = psum_mm.tile([P, BANK], F32, name="acc%d" % block)
-                    nc.tensor.matmul_mx(
-                        out=acc[:],
-                        lhsT=x_codes[:, j * P : (j + 1) * P].bitcast(FP8X4),
-                        lhsT_scale=x_scales[:, j * P : (j + 1) * P],
-                        rhs=w_codes[:, block * BANK : (block + 1) * BANK].bitcast(FP8X4),
-                        rhs_scale=w_scales[:, block * BANK : (block + 1) * BANK],
-                        start=True,
-                        stop=True,
-                    )
-                    banks.append(acc)
-                low = banks[0][:].rearrange("p (n d) -> p n d", d=HALF)
-                high = banks[1][:].rearrange("p (n d) -> p n d", d=HALF)
+            for pair in range(GROUP // PAIR):
+                rounds = slice(pair * PAIR, (pair + 1) * PAIR)
+                qk_cross = results.tile([P, QK_HEADS, PAIR, D], F32, name="qk_cross")
+                for i in range(PAIR):
+                    j = pair * PAIR + i
+                    banks = []
+                    for block in range(3):
+                        acc = psum_mm.tile([P, BANK], F32, name="acc%d" % block)
+                        nc.tensor.matmul_mx(
+                            out=acc[:],
+                            lhsT=x_codes[:, j * P : (j + 1) * P].bitcast(FP8X4),
+                            lhsT_scale=x_scales[:, j * P : (j + 1) * P],
+                            rhs=w_codes[:, block * BANK : (block + 1) * BANK].bitcast(FP8X4),
+                            rhs_scale=w_scales[:, block * BANK : (block + 1) * BANK],
+                            start=True,
+                            stop=True,
+                        )
+                        banks.append(acc)
+                    low = banks[0][:].rearrange("p (n d) -> p n d", d=HALF)
+                    high = banks[1][:].rearrange("p (n d) -> p n d", d=HALF)
 
-                def table(tab, first):
-                    return tab[:, j : j + 1, first : first + HALF].to_broadcast([P, QK_HEADS, HALF])
+                    def table(tab, first):
+                        return tab[:, j : j + 1, first : first + HALF].to_broadcast([P, QK_HEADS, HALF])
 
-                nc.vector.tensor_tensor(out=qk_main[:, :, j, 0:HALF], in0=low, in1=table(cos_g, 0), op=MULT)
-                nc.vector.tensor_tensor(out=qk_cross[:, :, i, HALF:D], in0=low, in1=table(sin_g, HALF), op=MULT)
-                nc.vector.tensor_tensor(out=qk_main[:, :, j, HALF:D], in0=high, in1=table(cos_g, HALF), op=MULT)
-                nc.vector.tensor_tensor(out=qk_cross[:, :, i, 0:HALF], in0=high, in1=table(sin_g, 0), op=MULT)
-                nc.scalar.copy(out=v_out[:, :, j, :], in_=banks[2][:].rearrange("p (h d) -> p h d", d=D))
+                    nc.vector.tensor_tensor(out=qk_main[:, :, j, 0:HALF], in0=low, in1=table(cos_g, 0), op=MULT)
+                    nc.vector.tensor_tensor(out=qk_cross[:, :, i, HALF:D], in0=low, in1=table(sin_g, HALF), op=MULT)
+                    nc.vector.tensor_tensor(out=qk_main[:, :, j, HALF:D], in0=high, in1=table(cos_g, HALF), op=MULT)
+                    nc.vector.tensor_tensor(out=qk_cross[:, :, i, 0:HALF], in0=high, in1=table(sin_g, 0), op=MULT)
+                    nc.scalar.copy(out=v_out[:, :, j, :], in_=banks[2][:].rearrange("p (h d) -> p h d", d=D))
 
-                if j == 1 and g + 1 < GROUPS:
+                if pair == 0 and not last_group:
                     codes_next = quantise_group(grouped_next)
-                if i == PAIR - 1:
-                    rounds = slice(j + 1 - PAIR, j + 1)
-                    nc.gpsimd.tensor_tensor(
-                        out=qk_main[:, :, rounds, 0:HALF],
-                        in0=qk_main[:, :, rounds, 0:HALF],
-                        in1=qk_cross[:, :, :, 0:HALF],
-                        op=SUBTRACT,
-                    )
-                    nc.gpsimd.tensor_tensor(
-                        out=qk_main[:, :, rounds, HALF:D],
-                        in0=qk_main[:, :, rounds, HALF:D],
-                        in1=qk_cross[:, :, :, HALF:D],
-                        op=ADD,
-                    )
-            nc.sync.dma_start(out=v_view[:, g], in_=v_out[:])
-            nc.sync.dma_start(out=q_view[:, g], in_=qk_main[:, 0:HEADS])
-            nc.sync.dma_start(out=k_view[:, g], in_=qk_main[:, HEADS:QK_HEADS])
+                adder = nc.vector if last_group and pair == GROUP // PAIR - 1 else nc.gpsimd
+                adder.tensor_tensor(
+                    out=qk_main[:, :, rounds, 0:HALF],
+                    in0=qk_main[:, :, rounds, 0:HALF],
+                    in1=qk_cross[:, :, :, 0:HALF],
+                    op=SUBTRACT,
+                )
+                adder.tensor_tensor(
+                    out=qk_main[:, :, rounds, HALF:D],
+                    in0=qk_main[:, :, rounds, HALF:D],
+                    in1=qk_cross[:, :, :, HALF:D],
+                    op=ADD,
+                )
+                if last_group:
+                    nc.sync.dma_start(out=v_view[:, g, :, rounds], in_=v_out[:, :, rounds])
+                    nc.sync.dma_start(out=q_view[:, g, :, rounds], in_=qk_main[:, 0:HEADS, rounds])
+                    nc.sync.dma_start(out=k_view[:, g, :, rounds], in_=qk_main[:, HEADS:QK_HEADS, rounds])
+            if not last_group:
+                nc.sync.dma_start(out=v_view[:, g], in_=v_out[:])
+                nc.sync.dma_start(out=q_view[:, g], in_=qk_main[:, 0:HEADS])
+                nc.sync.dma_start(out=k_view[:, g], in_=qk_main[:, HEADS:QK_HEADS])

@@ -55,18 +55,16 @@ def tile_swaattention_pa_t_kernel(tc, x, freqs_cos, freqs_sin, w_attn, out_0, ou
             in_=w_attn.rearrange("(u p e) c -> p u (e c)", u=2, p=P, e=2),
         )
         x_in = []
-        cos_in = []
-        sin_in = []
+        tables_in = []
         for g in range(GROUPS):
             x_g = inputs.tile([P, GROUP * C], BF16, name="x_g")
             nc.sync.dma_start(out=x_g[:], in_=x_view[:, g, :])
-            cos_g = inputs.tile([P, GROUP, D], BF16, name="cos_g")
-            nc.sync.dma_start(out=cos_g[:], in_=cos_view[:, g])
-            sin_g = inputs.tile([P, GROUP, D], BF16, name="sin_g")
-            nc.sync.dma_start(out=sin_g[:], in_=sin_view[:, g])
+            tables_g = inputs.tile([P, 2, GROUP, D], BF16, name="tables_g")
+            nc.sync.dma_start(out=tables_g[:, 0], in_=cos_view[:, g])
+            nc.sync.dma_start(out=tables_g[:, 1, :, 0:HALF], in_=sin_view[:, g, :, HALF:D])
+            nc.sync.dma_start(out=tables_g[:, 1, :, HALF:D], in_=sin_view[:, g, :, 0:HALF])
             x_in.append(x_g)
-            cos_in.append(cos_g)
-            sin_in.append(sin_g)
+            tables_in.append(tables_g)
 
         identity = const.tile([P, P], F32)
         make_identity(nc, identity[:])
@@ -131,15 +129,14 @@ def tile_swaattention_pa_t_kernel(tc, x, freqs_cos, freqs_sin, w_attn, out_0, ou
             x_codes, x_scales = codes_next
             if not last_group:
                 grouped_next = transpose_group(g + 1)
-            cos_g = cos_in[g]
-            sin_g = sin_in[g]
-            qk_main = results.tile([P, QK_HEADS, GROUP, D], F32, name="qk_main")
+            tables_g = tables_in[g]
+            products = results.tile([P, 2, QK_HEADS, GROUP, D], F32, name="products")
+            rotated = products[:, 0]
+            crossed = products[:, 1]
             v_out = results.tile([P, HEADS, GROUP, D], F32, name="v_out")
             for pair in range(GROUP // PAIR):
                 rounds = slice(pair * PAIR, (pair + 1) * PAIR)
-                qk_cross = results.tile([P, QK_HEADS, PAIR, D], F32, name="qk_cross")
-                for i in range(PAIR):
-                    j = pair * PAIR + i
+                for j in range(pair * PAIR, (pair + 1) * PAIR):
                     banks = []
                     for block in range(3):
                         acc = psum_mm.tile([P, BANK], F32, name="acc%d" % block)
@@ -153,38 +150,39 @@ def tile_swaattention_pa_t_kernel(tc, x, freqs_cos, freqs_sin, w_attn, out_0, ou
                             stop=True,
                         )
                         banks.append(acc)
-                    low = banks[0][:].rearrange("p (n d) -> p n d", d=HALF)
-                    high = banks[1][:].rearrange("p (n d) -> p n d", d=HALF)
-
-                    def table(tab, first):
-                        return tab[:, j : j + 1, first : first + HALF].to_broadcast([P, QK_HEADS, HALF])
-
-                    nc.vector.tensor_tensor(out=qk_main[:, :, j, 0:HALF], in0=low, in1=table(cos_g, 0), op=MULT)
-                    nc.vector.tensor_tensor(out=qk_cross[:, :, i, HALF:D], in0=low, in1=table(sin_g, HALF), op=MULT)
-                    nc.vector.tensor_tensor(out=qk_main[:, :, j, HALF:D], in0=high, in1=table(cos_g, HALF), op=MULT)
-                    nc.vector.tensor_tensor(out=qk_cross[:, :, i, 0:HALF], in0=high, in1=table(sin_g, 0), op=MULT)
+                    for f in range(2):
+                        columns = slice(f * HALF, (f + 1) * HALF)
+                        nc.vector.tensor_tensor(
+                            out=products[:, :, :, j, columns],
+                            in0=banks[f][:]
+                            .rearrange("p (n d) -> p n d", d=HALF)
+                            .unsqueeze(1)
+                            .to_broadcast([P, 2, QK_HEADS, HALF]),
+                            in1=tables_g[:, :, j, columns].unsqueeze(2).to_broadcast([P, 2, QK_HEADS, HALF]),
+                            op=MULT,
+                        )
                     nc.scalar.copy(out=v_out[:, :, j, :], in_=banks[2][:].rearrange("p (h d) -> p h d", d=D))
 
                 if pair == 0 and not last_group:
                     codes_next = quantise_group(grouped_next)
                 adder = nc.vector if last_group and pair == GROUP // PAIR - 1 else nc.gpsimd
                 adder.tensor_tensor(
-                    out=qk_main[:, :, rounds, 0:HALF],
-                    in0=qk_main[:, :, rounds, 0:HALF],
-                    in1=qk_cross[:, :, :, 0:HALF],
+                    out=rotated[:, :, rounds, 0:HALF],
+                    in0=rotated[:, :, rounds, 0:HALF],
+                    in1=crossed[:, :, rounds, HALF:D],
                     op=SUBTRACT,
                 )
                 adder.tensor_tensor(
-                    out=qk_main[:, :, rounds, HALF:D],
-                    in0=qk_main[:, :, rounds, HALF:D],
-                    in1=qk_cross[:, :, :, HALF:D],
+                    out=rotated[:, :, rounds, HALF:D],
+                    in0=rotated[:, :, rounds, HALF:D],
+                    in1=crossed[:, :, rounds, 0:HALF],
                     op=ADD,
                 )
                 if last_group:
                     nc.sync.dma_start(out=v_view[:, g, :, rounds], in_=v_out[:, :, rounds])
-                    nc.sync.dma_start(out=q_view[:, g, :, rounds], in_=qk_main[:, 0:HEADS, rounds])
-                    nc.sync.dma_start(out=k_view[:, g, :, rounds], in_=qk_main[:, HEADS:QK_HEADS, rounds])
+                    nc.sync.dma_start(out=q_view[:, g, :, rounds], in_=rotated[:, 0:HEADS, rounds])
+                    nc.sync.dma_start(out=k_view[:, g, :, rounds], in_=rotated[:, HEADS:QK_HEADS, rounds])
             if not last_group:
                 nc.sync.dma_start(out=v_view[:, g], in_=v_out[:])
-                nc.sync.dma_start(out=q_view[:, g], in_=qk_main[:, 0:HEADS])
-                nc.sync.dma_start(out=k_view[:, g], in_=qk_main[:, HEADS:QK_HEADS])
+                nc.sync.dma_start(out=q_view[:, g], in_=rotated[:, 0:HEADS])
+                nc.sync.dma_start(out=k_view[:, g], in_=rotated[:, HEADS:QK_HEADS])

from contextlib import ExitStack

import concourse.mybir as mybir
from concourse.masks import make_identity

F32 = mybir.dt.float32
BF16 = mybir.dt.bfloat16
U32 = mybir.dt.uint32
U8 = mybir.dt.uint8
FP8X4 = mybir.dt.float8_e4m3fn_x4
MULT = mybir.AluOpType.mult
ADD = mybir.AluOpType.add
SUBTRACT = mybir.AluOpType.subtract

P = 128
T = 4096
C = 512
PACK = 4
HEADS = 4
D = 128
HALF = D // 2
QK_HEADS = 2 * HEADS
BANK = 512

ROUNDS = T // P
GROUP = 4
GROUPS = ROUNDS // GROUP
PAIR = 2

FLOPS = 2 * T * C * 3 * C


def tile_swaattention_pa_t_kernel(tc, x, freqs_cos, freqs_sin, w_attn, out_0, out_1, out_2):
    nc = tc.nc

    x_view = x.rearrange("b (p g j) c -> (b p) g (j c)", g=GROUPS, j=GROUP)
    cos_view = freqs_cos.rearrange("(p g j) d -> p g j d", g=GROUPS, j=GROUP)
    sin_view = freqs_sin.rearrange("(p g j) d -> p g j d", g=GROUPS, j=GROUP)
    q_view = out_0.rearrange("b h (p g j) d -> p g (b h) j d", g=GROUPS, j=GROUP)
    k_view = out_1.rearrange("b h (p g j) d -> p g (b h) j d", g=GROUPS, j=GROUP)
    v_view = out_2.rearrange("b h (p g j) d -> p g (b h) j d", g=GROUPS, j=GROUP)

    with ExitStack() as ctx:
        ctx.enter_context(tc.manual_schedule())
        const = ctx.enter_context(tc.tile_pool(name="const", bufs=1))
        inputs = ctx.enter_context(tc.tile_pool(name="inputs", bufs=GROUPS))
        xq = ctx.enter_context(tc.tile_pool(name="xq", bufs=2))
        results = ctx.enter_context(tc.tile_pool(name="results", bufs=3))
        psum_t = ctx.enter_context(tc.psum_pool(name="psum_t", bufs=2))
        psum_mm = ctx.enter_context(tc.psum_pool(name="psum_mm", bufs=2))

        w_raw = const.tile([P, PACK, 3 * C], BF16)
        nc.sync.dma_start(
            out=w_raw[:].rearrange("p (u e) c -> p u (e c)", u=2),
            in_=w_attn.rearrange("(u p e) c -> p u (e c)", u=2, p=P, e=2),
        )
        x_in = []
        tables_in = []
        for g in range(GROUPS):
            x_g = inputs.tile([P, GROUP * C], BF16, name="x_g")
            nc.sync.dma_start(out=x_g[:], in_=x_view[:, g, :])
            tables_g = inputs.tile([P, 2, GROUP, D], BF16, name="tables_g")
            nc.sync.dma_start(out=tables_g[:, 0], in_=cos_view[:, g])
            nc.sync.dma_start(out=tables_g[:, 1, :, 0:HALF], in_=sin_view[:, g, :, HALF:D])
            nc.sync.dma_start(out=tables_g[:, 1, :, HALF:D], in_=sin_view[:, g, :, 0:HALF])
            x_in.append(x_g)
            tables_in.append(tables_g)

        identity = const.tile([P, P], F32)
        make_identity(nc, identity[:])

        def transpose_group(g):
            x_words = x_in[g][:].bitcast(F32)
            grouped = xq.tile([P, GROUP * P * PACK], BF16, name="grouped", align_bytes=64)
            grouped_words = grouped[:].bitcast(F32).rearrange(
                "p (j r u) -> p j r u", j=GROUP, r=P, u=2
            )
            for half_group in range(GROUP // 2):
                turned = psum_t.tile([P, 2, 2, P], F32, name="turned")
                for i in range(2):
                    j = 2 * half_group + i
                    for u in range(2):
                        first = (2 * j + u) * P
                        nc.tensor.transpose(turned[:, i, u, :], x_words[:, first : first + P], identity[:])
                nc.scalar.copy(
                    out=grouped_words[:, 2 * half_group : 2 * half_group + 2],
                    in_=turned[:].rearrange("p i u r -> p i r u"),
                )
            return grouped

        def quantise_group(grouped):
            x_codes = xq.tile([P, GROUP * P], U32, name="x_codes", align_bytes=64)
            x_scales = xq.tile([P, GROUP * P], U8, name="x_scales", align_bytes=64)
            nc.vector.quantize_mx(out=x_codes[:].bitcast(FP8X4), scales=x_scales[:], in_=grouped[:])
            return x_codes, x_scales

        w_grouped = const.tile([P, 3 * BANK * PACK], BF16, align_bytes=64)
        w_codes = const.tile([P, 3 * BANK], U32, align_bytes=64)
        w_scales = const.tile([P, 3 * BANK], U8, align_bytes=64)
        qk_halves = w_raw[:, :, 0 : 2 * C].rearrange("p t (n f d) -> p f n d t", f=2, d=HALF)

        grouped_next = transpose_group(0)
        for f in range(2):
            nc.vector.tensor_copy(
                out=w_grouped[:, f * BANK * PACK : (f + 1) * BANK * PACK].rearrange(
                    "p (n d t) -> p n d t", n=QK_HEADS, d=HALF
                ),
                in_=qk_halves[:, f],
            )
        nc.scalar.copy(
            out=w_grouped[:, 2 * BANK * PACK : 3 * BANK * PACK].rearrange("p (c t) -> p c t", t=PACK),
            in_=w_raw[:, :, 2 * C : 3 * C].rearrange("p t c -> p c t"),
        )
        for block in (0, 1):
            nc.vector.quantize_mx(
                out=w_codes[:, block * BANK : (block + 1) * BANK].bitcast(FP8X4),
                scales=w_scales[:, block * BANK : (block + 1) * BANK],
                in_=w_grouped[:, block * BANK * PACK : (block + 1) * BANK * PACK],
            )
        codes_next = quantise_group(grouped_next)
        nc.vector.quantize_mx(
            out=w_codes[:, 2 * BANK : 3 * BANK].bitcast(FP8X4),
            scales=w_scales[:, 2 * BANK : 3 * BANK],
            in_=w_grouped[:, 2 * BANK * PACK : 3 * BANK * PACK],
        )

        for g in range(GROUPS):
            last_group = g == GROUPS - 1
            x_codes, x_scales = codes_next
            if not last_group:
                grouped_next = transpose_group(g + 1)
            tables_g = tables_in[g]
            products = results.tile([P, 2, QK_HEADS, GROUP, D], F32, name="products")
            rotated = products[:, 0]
            crossed = products[:, 1]
            v_out = results.tile([P, HEADS, GROUP, D], F32, name="v_out")
            for pair in range(GROUP // PAIR):
                rounds = slice(pair * PAIR, (pair + 1) * PAIR)
                for j in range(pair * PAIR, (pair + 1) * PAIR):
                    banks = []
                    for block in range(3):
                        acc = psum_mm.tile([P, BANK], F32, name="acc%d" % block)
                        nc.tensor.matmul_mx(
                            out=acc[:],
                            lhsT=x_codes[:, j * P : (j + 1) * P].bitcast(FP8X4),
                            lhsT_scale=x_scales[:, j * P : (j + 1) * P],
                            rhs=w_codes[:, block * BANK : (block + 1) * BANK].bitcast(FP8X4),
                            rhs_scale=w_scales[:, block * BANK : (block + 1) * BANK],
                            start=True,
                            stop=True,
                        )
                        banks.append(acc)
                    for f in range(2):
                        columns = slice(f * HALF, (f + 1) * HALF)
                        nc.vector.tensor_tensor(
                            out=products[:, :, :, j, columns],
                            in0=banks[f][:]
                            .rearrange("p (n d) -> p n d", d=HALF)
                            .unsqueeze(1)
                            .to_broadcast([P, 2, QK_HEADS, HALF]),
                            in1=tables_g[:, :, j, columns].unsqueeze(2).to_broadcast([P, 2, QK_HEADS, HALF]),
                            op=MULT,
                        )
                    nc.scalar.copy(out=v_out[:, :, j, :], in_=banks[2][:].rearrange("p (h d) -> p h d", d=D))

                if pair == 0 and not last_group:
                    codes_next = quantise_group(grouped_next)
                adder = nc.vector if last_group and pair == GROUP // PAIR - 1 else nc.gpsimd
                adder.tensor_tensor(
                    out=rotated[:, :, rounds, 0:HALF],
                    in0=rotated[:, :, rounds, 0:HALF],
                    in1=crossed[:, :, rounds, HALF:D],
                    op=SUBTRACT,
                )
                adder.tensor_tensor(
                    out=rotated[:, :, rounds, HALF:D],
                    in0=rotated[:, :, rounds, HALF:D],
                    in1=crossed[:, :, rounds, 0:HALF],
                    op=ADD,
                )
                if last_group:
                    nc.sync.dma_start(out=v_view[:, g, :, rounds], in_=v_out[:, :, rounds])
                    nc.sync.dma_start(out=q_view[:, g, :, rounds], in_=rotated[:, 0:HEADS, rounds])
                    nc.sync.dma_start(out=k_view[:, g, :, rounds], in_=rotated[:, HEADS:QK_HEADS, rounds])
            if not last_group:
                nc.sync.dma_start(out=v_view[:, g], in_=v_out[:])
                nc.sync.dma_start(out=q_view[:, g], in_=rotated[:, 0:HEADS])
                nc.sync.dma_start(out=k_view[:, g], in_=rotated[:, HEADS:QK_HEADS])
